import numpy as np
import ml_dtypes


def mxq(x, axis, fmt="e4m3"):
    dtype, down = {"e4m3": (ml_dtypes.float8_e4m3fn, 7), "e5m2": (ml_dtypes.float8_e5m2, 14)}[fmt]
    v = np.moveaxis(np.asarray(x, np.float32).astype(ml_dtypes.bfloat16).astype(np.float64), axis, -1)
    blocks = v.reshape(v.shape[:-1] + (-1, 32))
    amax = np.abs(blocks).max(-1, keepdims=True)
    byte = np.maximum(np.where(amax > 0, np.frexp(amax)[1] - 1 + 127, 0) - down, 1)
    scale = np.exp2(byte - 127.0)
    codes = (blocks / scale).astype(np.float32).astype(dtype).astype(np.float64)
    return np.moveaxis((codes * scale).reshape(v.shape), -1, axis)


WIDE = False


def mx_kscale(k):
    if not WIDE:
        return np.ones(k)
    levels = np.array([10, -10, 5, -5, 0])
    a = np.random.permutation(np.resize(levels, k // 512 * 4)).reshape(k // 512, 4)
    idx = np.arange(k)
    return np.exp2(a[idx // 512, idx % 128 // 32])


BF16 = ml_dtypes.bfloat16


def bf(x):
    return np.asarray(x, np.float32).astype(BF16)


def f64(x):
    return np.asarray(x).astype(np.float64)


B, S, D, H, DK, R = 2, 512, 1024, 16, 64, 32
A = 1.0 / np.sqrt(np.sqrt(S))


def setup_inputs():
    sk, se = mx_kscale(D), mx_kscale(D)
    n = np.random.standard_normal
    return {"k": bf(n((B, S, D)) * sk),
            "e": bf(n((B, S, D)) * se),
            "Wk": bf(n((D, H * DK)) * A / np.sqrt(D) / sk[:, None]),
            "bk": bf(n(H * DK) * 0.1 * A),
            "We": bf(n((D, H * R)) * A / np.sqrt(D) / se[:, None]),
            "be": bf(n(H * R) * 0.1 * A)}


def reference(k, e, Wk, bk, We, be):
    kh = ((mxq(f64(k), 2, "e4m3") @ mxq(f64(Wk), 0, "e4m3")) + f64(bk)).reshape(B, S, H, DK)
    eh = ((mxq(f64(e), 2, "e4m3") @ mxq(f64(We), 0, "e4m3")) + f64(be)).reshape(B, S, H, R)
    return mxq(eh.transpose(0, 2, 3, 1), 3, "e4m3") @ mxq(kh.transpose(0, 2, 1, 3), 2, "e4m3")

@@ -1,0 +1,221 @@
+from contextlib import ExitStack
+
+import concourse.mybir as mybir
+from concourse.masks import make_identity
+
+BF16 = mybir.dt.bfloat16
+F32 = mybir.dt.float32
+U32 = mybir.dt.uint32
+U8 = mybir.dt.uint8
+FP8X4 = mybir.dt.float8_e4m3fn_x4
+ADD = mybir.AluOpType.add
+
+BATCH = 2
+SEQ = 512
+MODEL = 1024
+HEADS = 16
+HEAD_DIM = 64
+SLOTS = 32
+
+P = 128
+PACK = 4
+K_PASS = P * PACK
+PASSES = MODEL // K_PASS
+TOKEN_TILES = SEQ // P
+CHUNK = 512
+BLOCK = 256
+HEADS_PER_PASS = P // SLOTS
+
+START_AHEAD = 2
+COMPRESS_LAG = 2
+
+FLOPS = 2 * BATCH * SEQ * MODEL * HEADS * (HEAD_DIM + SLOTS) + 2 * BATCH * HEADS * SLOTS * HEAD_DIM * SEQ
+
+
+def tile_multiheadattention_pa_kernel(tc, k, e, Wk, bk, We, be, out):
+    nc = tc.nc
+    with ExitStack() as ctx:
+        const = ctx.enter_context(tc.tile_pool(name="const", bufs=1))
+        raw = ctx.enter_context(tc.tile_pool(name="raw", bufs=1))
+        grouped = ctx.enter_context(tc.tile_pool(name="grouped", bufs=4))
+        quantised = ctx.enter_context(tc.tile_pool(name="quantised", bufs=1))
+        psum_flip = ctx.enter_context(tc.psum_pool(name="psum_flip", bufs=2))
+        psum_acc = ctx.enter_context(tc.psum_pool(name="psum_acc", bufs=4))
+        psum_kc = ctx.enter_context(tc.psum_pool(name="psum_kc", bufs=2))
+
+        identity = const.tile([P, P], F32)
+        make_identity(nc, identity[:])
+        ones = const.tile([P, P], BF16)
+        nc.vector.memset(ones[:], 1.0)
+        bias_cols = 3 * CHUNK
+        bias_rows = const.tile([P, bias_cols], BF16)
+        nc.vector.memset(bias_rows[:], 0.0)
+
+        nc.sync.dma_start(out=bias_rows[0:1, 0:CHUNK], in_=be.rearrange("(o c) -> o c", o=1))
+        nc.sync.dma_start(out=bias_rows[0:1, CHUNK:bias_cols], in_=bk.rearrange("(o c) -> o c", o=1))
+
+        def load_weight_chunk(w, col0, name):
+            w_raw = raw.tile([P, PASSES, PACK, CHUNK], BF16, name=name)
+            for g in range(PASSES):
+                for u in range(2):
+                    row0 = K_PASS * g + 2 * P * u
+                    nc.sync.dma_start(
+                        out=w_raw[:, g, 2 * u : 2 * u + 2, :],
+                        in_=w[row0 : row0 + 2 * P, col0 : col0 + CHUNK].rearrange("(q e) c -> q e c", e=2),
+                    )
+            return w_raw
+
+        def load_tokens(x, b, name):
+            by_tile = x[b].rearrange("(p j) d -> j p d", j=TOKEN_TILES)
+            tiles = []
+            for j in range(TOKEN_TILES):
+                x_raw = raw.tile([P, MODEL], BF16, name="%s%d%d" % (name, b, j))
+                nc.sync.dma_start(out=x_raw[:], in_=by_tile[j])
+                tiles.append(x_raw)
+            return tiles
+
+        w_raws = {}
+        x_raws = {}
+        w_raws[0] = load_weight_chunk(We, 0, "we_raw")
+        x_raws[(0, 0)] = load_tokens(e, 0, "e_raw")
+        x_raws[(0, 1)] = load_tokens(e, 1, "e_raw")
+        w_raws[1] = load_weight_chunk(Wk, 0, "wk_raw0")
+        x_raws[(1, 0)] = load_tokens(k, 0, "k_raw")
+        x_raws[(1, 1)] = load_tokens(k, 1, "k_raw")
+        w_raws[2] = load_weight_chunk(Wk, CHUNK, "wk_raw1")
+
+        bias = const.tile([P, bias_cols], F32)
+        for c in range(3):
+            spread = psum_acc.tile([P, CHUNK], F32, tag="acc")
+            nc.tensor.matmul(
+                out=spread[:], lhsT=ones[:], rhs=bias_rows[:, c * CHUNK : (c + 1) * CHUNK], start=True, stop=True
+            )
+            nc.vector.tensor_copy(out=bias[:, c * CHUNK : (c + 1) * CHUNK], in_=spread[:])
+
+        result = const.tile([P, BATCH, HEADS // HEADS_PER_PASS, BLOCK], F32)
+
+        def quantise(values, name):
+            words = values.shape[1] // PACK
+            codes = quantised.tile([P, words], U32, name=name + "_codes", align_bytes=64)
+            scales = quantised.tile([P, words], U8, name=name + "_scales", align_bytes=64)
+            nc.vector.quantize_mx(out=codes[:].bitcast(FP8X4), scales=scales[:], in_=values)
+            return codes, scales
+
+        def mx_pass(acc, stationary, s_col, moving, m_col, width, start, stop):
+            nc.tensor.matmul_mx(
+                out=acc,
+                lhsT=stationary[0][:, s_col : s_col + P].bitcast(FP8X4),
+                lhsT_scale=stationary[1][:, s_col : s_col + P],
+                rhs=moving[0][:, m_col : m_col + width].bitcast(FP8X4),
+                rhs_scale=moving[1][:, m_col : m_col + width],
+                start=start,
+                stop=stop,
+            )
+
+        def regroup_weights(c, blk):
+            w_grouped = grouped.tile([P, PASSES, BLOCK, PACK], BF16, align_bytes=64)
+            for g in range(PASSES):
+                dst = w_grouped[:, g].rearrange("p (c i) t -> p c t i", i=4)
+                src = w_raws[c][:, g, :, blk * BLOCK : (blk + 1) * BLOCK].rearrange("p t (c i) -> p c t i", i=4)
+                if c == 0 and blk == 0:
+                    nc.vector.tensor_copy(out=dst, in_=src)
+                else:
+                    nc.scalar.copy(out=dst, in_=src)
+            return w_grouped
+
+        def transpose_tokens(tiles):
+            pairs = []
+            for first in range(0, TOKEN_TILES, 2):
+                x_grouped = grouped.tile([P, 2 * MODEL], BF16, align_bytes=64)
+                x_words = x_grouped[:].bitcast(F32).rearrange("p (j g w u) -> p j g w u", j=2, g=PASSES, u=2)
+                for j in range(2):
+                    token_words = tiles[first + j][:].bitcast(F32)
+                    flipped = psum_flip.tile([P, 2 * PASSES, P], F32)
+                    for q in range(2 * PASSES):
+                        nc.tensor.transpose(flipped[:, q, :], token_words[:, q * P : (q + 1) * P], identity[:])
+                    nc.scalar.copy(out=x_words[:, j], in_=flipped[:].rearrange("p (g u) w -> p g w u", u=2))
+                pairs.append(x_grouped)
+            return pairs
+
+        def project(x_pairs, w_block, bias_col, name):
+            h_grouped = grouped.tile([P, BLOCK, PACK], BF16, align_bytes=64)
+            for half in range(BLOCK // P):
+                acc = psum_acc.tile([P, TOKEN_TILES, P], F32, tag="acc")
+                for j in range(TOKEN_TILES):
+                    for g in range(PASSES):
+                        mx_pass(
+                            acc[:, j, :],
+                            x_pairs[j // 2],
+                            ((j % 2) * PASSES + g) * P,
+                            w_block,
+                            g * BLOCK + half * P,
+                            P,
+                            g == 0,
+                            g == PASSES - 1,
+                        )
+                col = bias_col + half * P
+                nc.vector.tensor_tensor(
+                    out=h_grouped[:, half * P : (half + 1) * P, :],
+                    in0=acc[:].rearrange("p j c -> p c j"),
+                    in1=bias[:, col : col + P].unsqueeze(2).to_broadcast([P, P, TOKEN_TILES]),
+                    op=ADD,
+                )
+            return quantise(h_grouped[:].rearrange("p c j -> p (c j)"), name)
+
+        def compress(c, b, blk):
+            kc = psum_kc.tile([P, BLOCK], F32)
+            mx_pass(kc[:], h_ready[(0, b, c - 1)], blk * P, h_ready[(c, b, blk)], 0, BLOCK, True, True)
+            nc.scalar.copy(out=result[:, b, 2 * (c - 1) + blk, :], in_=kc[:])
+
+        steps = [(c, b, blk) for c in range(3) for b in range(BATCH) for blk in range(CHUNK // BLOCK)]
+        w_grouped_of = {}
+        x_grouped_of = {}
+        w_ready = {}
+        x_ready = {}
+        h_ready = {}
+
+        def start(step):
+            c, b, blk = step
+            stream = min(c, 1)
+            if (c, blk) not in w_grouped_of:
+                w_grouped_of[(c, blk)] = regroup_weights(c, blk)
+            if (stream, b) not in x_grouped_of:
+                x_grouped_of[(stream, b)] = transpose_tokens(x_raws[(stream, b)])
+
+        def finish(step):
+            c, b, blk = step
+            stream = min(c, 1)
+            if (c, blk) not in w_ready:
+                w_ready[(c, blk)] = quantise(
+                    w_grouped_of[(c, blk)][:].rearrange("p g c t -> p (g c t)"), "w%d%d" % (c, blk)
+                )
+            if (stream, b) not in x_ready:
+                x_ready[(stream, b)] = [
+                    quantise(pair[:], "x%d%d%d" % (stream, b, n)) for n, pair in enumerate(x_grouped_of[(stream, b)])
+                ]
+
+        for n in range(START_AHEAD):
+            start(steps[n])
+        finish(steps[0])
+        for n, step in enumerate(steps):
+            c, b, blk = step
+            if n + START_AHEAD < len(steps):
+                start(steps[n + START_AHEAD])
+            if n + 1 < len(steps):
+                finish(steps[n + 1])
+            h_ready[step] = project(
+                x_ready[(min(c, 1), b)], w_ready[(c, blk)], c * CHUNK + blk * BLOCK, "h%d%d%d" % step
+            )
+            if n >= COMPRESS_LAG and steps[n - COMPRESS_LAG][0] > 0:
+                compress(*steps[n - COMPRESS_LAG])
+        for step in steps[len(steps) - COMPRESS_LAG :]:
+            compress(*step)
+
+        by_quadrant = out.rearrange("b (hg i) r d -> i r (b hg) d", i=HEADS_PER_PASS)
+        for i in range(HEADS_PER_PASS):
+            nc.sync.dma_start(
+                out=by_quadrant[i],
+                in_=result[i * SLOTS : (i + 1) * SLOTS].rearrange("p b hg c -> p (b hg) c")[
+                    :, :, i * HEAD_DIM : (i + 1) * HEAD_DIM
+                ],
+            )

@@ -26,8 +26,9 @@ CHUNK = 512
 BLOCK = 256
 HEADS_PER_PASS = P // SLOTS
 
-START_AHEAD = 2
-COMPRESS_LAG = 2
+TOKENS_AHEAD = 2
+WEIGHTS_AHEAD = 3
+COMPRESS_LAG = 3
 
 FLOPS = 2 * BATCH * SEQ * MODEL * HEADS * (HEAD_DIM + SLOTS) + 2 * BATCH * HEADS * SLOTS * HEAD_DIM * SEQ
 
@@ -35,24 +36,25 @@ FLOPS = 2 * BATCH * SEQ * MODEL * HEADS * (HEAD_DIM + SLOTS) + 2 * BATCH * HEADS
 def tile_multiheadattention_pa_kernel(tc, k, e, Wk, bk, We, be, out):
     nc = tc.nc
     with ExitStack() as ctx:
+        ctx.enter_context(tc.manual_schedule())
         const = ctx.enter_context(tc.tile_pool(name="const", bufs=1))
         raw = ctx.enter_context(tc.tile_pool(name="raw", bufs=1))
         grouped = ctx.enter_context(tc.tile_pool(name="grouped", bufs=4))
         quantised = ctx.enter_context(tc.tile_pool(name="quantised", bufs=1))
-        psum_flip = ctx.enter_context(tc.psum_pool(name="psum_flip", bufs=2))
-        psum_acc = ctx.enter_context(tc.psum_pool(name="psum_acc", bufs=4))
-        psum_kc = ctx.enter_context(tc.psum_pool(name="psum_kc", bufs=2))
+        psum_flip = ctx.enter_context(tc.psum_pool(name="psum_flip", bufs=4))
+        psum_acc = ctx.enter_context(tc.psum_pool(name="psum_acc", bufs=3))
+        psum_kc = ctx.enter_context(tc.psum_pool(name="psum_kc", bufs=1))
 
         identity = const.tile([P, P], F32)
         make_identity(nc, identity[:])
-        ones = const.tile([P, P], BF16)
-        nc.vector.memset(ones[:], 1.0)
         bias_cols = 3 * CHUNK
         bias_rows = const.tile([P, bias_cols], BF16)
-        nc.vector.memset(bias_rows[:], 0.0)
+        nc.vector.memset(bias_rows[:].bitcast(mybir.dt.int32), 0)
+        ones = const.tile([P, P], BF16)
+        nc.vector.memset(ones[:], 1.0)
 
-        nc.sync.dma_start(out=bias_rows[0:1, 0:CHUNK], in_=be.rearrange("(o c) -> o c", o=1))
-        nc.sync.dma_start(out=bias_rows[0:1, CHUNK:bias_cols], in_=bk.rearrange("(o c) -> o c", o=1))
+        nc.scalar.dma_start(out=bias_rows[0:1, 0:CHUNK], in_=be.rearrange("(o c) -> o c", o=1))
+        nc.scalar.dma_start(out=bias_rows[0:1, CHUNK:bias_cols], in_=bk.rearrange("(o c) -> o c", o=1))
 
         def load_weight_chunk(w, col0, name):
             w_raw = raw.tile([P, PASSES, PACK, CHUNK], BF16, name=name)
@@ -85,12 +87,13 @@ def tile_multiheadattention_pa_kernel(tc, k, e, Wk, bk, We, be, out):
         w_raws[2] = load_weight_chunk(Wk, CHUNK, "wk_raw1")
 
         bias = const.tile([P, bias_cols], F32)
-        for c in range(3):
-            spread = psum_acc.tile([P, CHUNK], F32, tag="acc")
+
+        def spread_bias(c):
+            spread = psum_flip.tile([P, CHUNK], F32, tag="flipped")
             nc.tensor.matmul(
                 out=spread[:], lhsT=ones[:], rhs=bias_rows[:, c * CHUNK : (c + 1) * CHUNK], start=True, stop=True
             )
-            nc.vector.tensor_copy(out=bias[:, c * CHUNK : (c + 1) * CHUNK], in_=spread[:])
+            nc.scalar.copy(out=bias[:, c * CHUNK : (c + 1) * CHUNK], in_=spread[:])
 
         result = const.tile([P, BATCH, HEADS // HEADS_PER_PASS, BLOCK], F32)
 
@@ -117,7 +120,7 @@ def tile_multiheadattention_pa_kernel(tc, k, e, Wk, bk, We, be, out):
             for g in range(PASSES):
                 dst = w_grouped[:, g].rearrange("p (c i) t -> p c t i", i=4)
                 src = w_raws[c][:, g, :, blk * BLOCK : (blk + 1) * BLOCK].rearrange("p t (c i) -> p c t i", i=4)
-                if c == 0 and blk == 0:
+                if c == 0:
                     nc.vector.tensor_copy(out=dst, in_=src)
                 else:
                     nc.scalar.copy(out=dst, in_=src)
@@ -130,37 +133,34 @@ def tile_multiheadattention_pa_kernel(tc, k, e, Wk, bk, We, be, out):
                 x_words = x_grouped[:].bitcast(F32).rearrange("p (j g w u) -> p j g w u", j=2, g=PASSES, u=2)
                 for j in range(2):
                     token_words = tiles[first + j][:].bitcast(F32)
-                    flipped = psum_flip.tile([P, 2 * PASSES, P], F32)
+                    flipped = psum_flip.tile([P, 2 * PASSES, P], F32, tag="flipped")
                     for q in range(2 * PASSES):
                         nc.tensor.transpose(flipped[:, q, :], token_words[:, q * P : (q + 1) * P], identity[:])
                     nc.scalar.copy(out=x_words[:, j], in_=flipped[:].rearrange("p (g u) w -> p g w u", u=2))
                 pairs.append(x_grouped)
             return pairs
 
-        def project(x_pairs, w_block, bias_col, name):
-            h_grouped = grouped.tile([P, BLOCK, PACK], BF16, align_bytes=64)
-            for half in range(BLOCK // P):
-                acc = psum_acc.tile([P, TOKEN_TILES, P], F32, tag="acc")
-                for j in range(TOKEN_TILES):
-                    for g in range(PASSES):
-                        mx_pass(
-                            acc[:, j, :],
-                            x_pairs[j // 2],
-                            ((j % 2) * PASSES + g) * P,
-                            w_block,
-                            g * BLOCK + half * P,
-                            P,
-                            g == 0,
-                            g == PASSES - 1,
-                        )
-                col = bias_col + half * P
-                nc.vector.tensor_tensor(
-                    out=h_grouped[:, half * P : (half + 1) * P, :],
-                    in0=acc[:].rearrange("p j c -> p c j"),
-                    in1=bias[:, col : col + P].unsqueeze(2).to_broadcast([P, P, TOKEN_TILES]),
-                    op=ADD,
-                )
-            return quantise(h_grouped[:].rearrange("p c j -> p (c j)"), name)
+        def project_half(x_pairs, w_block, bias_col, h_grouped, half):
+            acc = psum_acc.tile([P, TOKEN_TILES, P], F32, tag="acc")
+            for j in range(TOKEN_TILES):
+                for g in range(PASSES):
+                    mx_pass(
+                        acc[:, j, :],
+                        x_pairs[j // 2],
+                        ((j % 2) * PASSES + g) * P,
+                        w_block,
+                        g * BLOCK + half * P,
+                        P,
+                        g == 0,
+                        g == PASSES - 1,
+                    )
+            col = bias_col + half * P
+            nc.vector.tensor_tensor(
+                out=h_grouped[:, half * P : (half + 1) * P, :],
+                in0=acc[:].rearrange("p j c -> p c j"),
+                in1=bias[:, col : col + P].unsqueeze(2).to_broadcast([P, P, TOKEN_TILES]),
+                op=ADD,
+            )
 
         def compress(c, b, blk):
             kc = psum_kc.tile([P, BLOCK], F32)
@@ -174,13 +174,18 @@ def tile_multiheadattention_pa_kernel(tc, k, e, Wk, bk, We, be, out):
         x_ready = {}
         h_ready = {}
 
-        def start(step):
+        def start_weights(step):
             c, b, blk = step
-            stream = min(c, 1)
             if (c, blk) not in w_grouped_of:
                 w_grouped_of[(c, blk)] = regroup_weights(c, blk)
+
+        def start_tokens(step):
+            c, b, blk = step
+            stream = min(c, 1)
             if (stream, b) not in x_grouped_of:
                 x_grouped_of[(stream, b)] = transpose_tokens(x_raws[(stream, b)])
+            if b == 0 and blk == 0:
+                spread_bias(c)
 
         def finish(step):
             c, b, blk = step
@@ -194,20 +199,34 @@ def tile_multiheadattention_pa_kernel(tc, k, e, Wk, bk, We, be, out):
                     quantise(pair[:], "x%d%d%d" % (stream, b, n)) for n, pair in enumerate(x_grouped_of[(stream, b)])
                 ]
 
-        for n in range(START_AHEAD):
-            start(steps[n])
+        for n in range(WEIGHTS_AHEAD):
+            start_weights(steps[n])
+        for n in range(TOKENS_AHEAD):
+            start_tokens(steps[n])
         finish(steps[0])
+        h_grouped_of = {}
+
+        def quantise_h(step):
+            h_ready[step] = quantise(h_grouped_of[step][:].rearrange("p c j -> p (c j)"), "h%d%d%d" % step)
+
         for n, step in enumerate(steps):
             c, b, blk = step
-            if n + START_AHEAD < len(steps):
-                start(steps[n + START_AHEAD])
+            if n + TOKENS_AHEAD < len(steps):
+                start_tokens(steps[n + TOKENS_AHEAD])
+            if n + WEIGHTS_AHEAD < len(steps):
+                start_weights(steps[n + WEIGHTS_AHEAD])
             if n + 1 < len(steps):
                 finish(steps[n + 1])
-            h_ready[step] = project(
-                x_ready[(min(c, 1), b)], w_ready[(c, blk)], c * CHUNK + blk * BLOCK, "h%d%d%d" % step
-            )
+            h_grouped = grouped.tile([P, BLOCK, PACK], BF16, align_bytes=64)
+            h_grouped_of[step] = h_grouped
+            operands = (x_ready[(min(c, 1), b)], w_ready[(c, blk)], c * CHUNK + blk * BLOCK, h_grouped)
+            project_half(*operands, 0)
+            if n >= 1:
+                quantise_h(steps[n - 1])
+            project_half(*operands, 1)
             if n >= COMPRESS_LAG and steps[n - COMPRESS_LAG][0] > 0:
                 compress(*steps[n - COMPRESS_LAG])
+        quantise_h(steps[len(steps) - 1])
         for step in steps[len(steps) - COMPRESS_LAG :]:
             compress(*step)
 

@@ -204,6 +204,7 @@ def tile_multiheadattention_pa_kernel(tc, k, e, Wk, bk, We, be, out):
         for n in range(TOKENS_AHEAD):
             start_tokens(steps[n])
         finish(steps[0])
+        finish(steps[1])
         h_grouped_of = {}
 
         def quantise_h(step):
@@ -215,15 +216,15 @@ def tile_multiheadattention_pa_kernel(tc, k, e, Wk, bk, We, be, out):
                 start_tokens(steps[n + TOKENS_AHEAD])
             if n + WEIGHTS_AHEAD < len(steps):
                 start_weights(steps[n + WEIGHTS_AHEAD])
-            if n + 1 < len(steps):
-                finish(steps[n + 1])
             h_grouped = grouped.tile([P, BLOCK, PACK], BF16, align_bytes=64)
             h_grouped_of[step] = h_grouped
             operands = (x_ready[(min(c, 1), b)], w_ready[(c, blk)], c * CHUNK + blk * BLOCK, h_grouped)
             project_half(*operands, 0)
+            project_half(*operands, 1)
             if n >= 1:
                 quantise_h(steps[n - 1])
-            project_half(*operands, 1)
+            if n + 2 < len(steps):
+                finish(steps[n + 2])
             if n >= COMPRESS_LAG and steps[n - COMPRESS_LAG][0] > 0:
                 compress(*steps[n - COMPRESS_LAG])
         quantise_h(steps[len(steps) - 1])

@@ -9,6 +9,7 @@ U32 = mybir.dt.uint32
 U8 = mybir.dt.uint8
 FP8X4 = mybir.dt.float8_e4m3fn_x4
 ADD = mybir.AluOpType.add
+IDENTITY = mybir.ActivationFunctionType.Identity
 
 BATCH = 2
 SEQ = 512
@@ -42,67 +43,93 @@ def tile_multiheadattention_pa_kernel(tc, k, e, Wk, bk, We, be, out):
         grouped = ctx.enter_context(tc.tile_pool(name="grouped", bufs=4))
         quantised = ctx.enter_context(tc.tile_pool(name="quantised", bufs=1))
         psum_flip = ctx.enter_context(tc.psum_pool(name="psum_flip", bufs=4))
-        psum_acc = ctx.enter_context(tc.psum_pool(name="psum_acc", bufs=3))
-        psum_kc = ctx.enter_context(tc.psum_pool(name="psum_kc", bufs=1))
+        psum_acc = ctx.enter_context(tc.psum_pool(name="psum_acc", bufs=4))
 
         identity = const.tile([P, P], F32)
         make_identity(nc, identity[:])
+        scratch = const.tile([P, 2], BF16)
         bias_cols = 3 * CHUNK
         bias_rows = const.tile([P, bias_cols], BF16)
         nc.vector.memset(bias_rows[:].bitcast(mybir.dt.int32), 0)
         ones = const.tile([P, P], BF16)
         nc.vector.memset(ones[:], 1.0)
-
         nc.scalar.dma_start(out=bias_rows[0:1, 0:CHUNK], in_=be.rearrange("(o c) -> o c", o=1))
         nc.scalar.dma_start(out=bias_rows[0:1, CHUNK:bias_cols], in_=bk.rearrange("(o c) -> o c", o=1))
+        nc.scalar.copy(out=scratch[:], in_=ones[:, 0:2])
 
-        def load_weight_chunk(w, col0, name):
-            w_raw = raw.tile([P, PASSES, PACK, CHUNK], BF16, name=name)
+        def load_weight_pass(w, w_raw, g, col0):
+            for u in range(2):
+                row0 = K_PASS * g + 2 * P * u
+                nc.sync.dma_start(
+                    out=w_raw[:, g, 2 * u : 2 * u + 2, :],
+                    in_=w[row0 : row0 + 2 * P, col0 : col0 + CHUNK].rearrange("(q e) c -> q e c", e=2),
+                )
+
+        def load_weight_chunk(w, w_raw, col0):
             for g in range(PASSES):
-                for u in range(2):
-                    row0 = K_PASS * g + 2 * P * u
-                    nc.sync.dma_start(
-                        out=w_raw[:, g, 2 * u : 2 * u + 2, :],
-                        in_=w[row0 : row0 + 2 * P, col0 : col0 + CHUNK].rearrange("(q e) c -> q e c", e=2),
-                    )
-            return w_raw
+                load_weight_pass(w, w_raw, g, col0)
 
-        def load_tokens(x, b, name):
+        def load_token_tiles(x, b, tiles, js):
             by_tile = x[b].rearrange("(p j) d -> j p d", j=TOKEN_TILES)
-            tiles = []
-            for j in range(TOKEN_TILES):
-                x_raw = raw.tile([P, MODEL], BF16, name="%s%d%d" % (name, b, j))
-                nc.sync.dma_start(out=x_raw[:], in_=by_tile[j])
-                tiles.append(x_raw)
-            return tiles
+            for j in js:
+                nc.sync.dma_start(out=tiles[j][:], in_=by_tile[j])
 
         w_raws = {}
         x_raws = {}
-        w_raws[0] = load_weight_chunk(We, 0, "we_raw")
-        x_raws[(0, 0)] = load_tokens(e, 0, "e_raw")
-        x_raws[(0, 1)] = load_tokens(e, 1, "e_raw")
-        w_raws[1] = load_weight_chunk(Wk, 0, "wk_raw0")
-        x_raws[(1, 0)] = load_tokens(k, 0, "k_raw")
-        x_raws[(1, 1)] = load_tokens(k, 1, "k_raw")
-        w_raws[2] = load_weight_chunk(Wk, CHUNK, "wk_raw1")
+        for c in range(3):
+            w_raws[c] = raw.tile([P, PASSES, PACK, CHUNK], BF16, name="w_raw%d" % c)
+        for stream in range(2):
+            for b in range(BATCH):
+                x_raws[(stream, b)] = [
+                    raw.tile([P, MODEL], BF16, name="x_raw%d%d%d" % (stream, b, j)) for j in range(TOKEN_TILES)
+                ]
+        load_weight_pass(We, w_raws[0], 0, 0)
+        load_token_tiles(e, 0, x_raws[(0, 0)], (0, 1))
+        load_weight_pass(We, w_raws[0], 1, 0)
+        load_token_tiles(e, 0, x_raws[(0, 0)], (2, 3))
+        load_token_tiles(e, 1, x_raws[(0, 1)], range(TOKEN_TILES))
+        load_weight_chunk(Wk, w_raws[1], 0)
+        load_token_tiles(k, 0, x_raws[(1, 0)], range(TOKEN_TILES))
+        load_token_tiles(k, 1, x_raws[(1, 1)], range(TOKEN_TILES))
+        load_weight_chunk(Wk, w_raws[2], CHUNK)
 
-        bias = const.tile([P, bias_cols], F32)
+        bias = const.tile([P, bias_cols], BF16)
 
         def spread_bias(c):
-            spread = psum_flip.tile([P, CHUNK], F32, tag="flipped")
+            spread = psum_flip.tile([P, CHUNK], BF16, tag="flipped")
             nc.tensor.matmul(
                 out=spread[:], lhsT=ones[:], rhs=bias_rows[:, c * CHUNK : (c + 1) * CHUNK], start=True, stop=True
             )
             nc.scalar.copy(out=bias[:, c * CHUNK : (c + 1) * CHUNK], in_=spread[:])
 
+        bias_col = const.tile([P, bias_cols // P, 2], F32)
+
+        def turn_bias(first, last):
+            turned = psum_flip.tile([P, last - first, 2], F32, tag="flipped")
+            for i in range(first, last):
+                nc.tensor.matmul(
+                    out=turned[:, i - first, :],
+                    lhsT=bias_rows[:, i * P : (i + 1) * P],
+                    rhs=ones[:, 0:2],
+                    start=True,
+                    stop=True,
+                )
+            nc.scalar.copy(out=bias_col[:, first:last, :], in_=turned[:])
+
         result = const.tile([P, BATCH, HEADS // HEADS_PER_PASS, BLOCK], F32)
 
-        def quantise(values, name):
-            words = values.shape[1] // PACK
+        def new_codes(words, name):
             codes = quantised.tile([P, words], U32, name=name + "_codes", align_bytes=64)
             scales = quantised.tile([P, words], U8, name=name + "_scales", align_bytes=64)
-            nc.vector.quantize_mx(out=codes[:].bitcast(FP8X4), scales=scales[:], in_=values)
             return codes, scales
+
+        def quantise(target, first, values):
+            words = values.shape[1] // PACK
+            nc.vector.quantize_mx(
+                out=target[0][:, first : first + words].bitcast(FP8X4),
+                scales=target[1][:, first : first + words],
+                in_=values,
+            )
 
         def mx_pass(acc, stationary, s_col, moving, m_col, width, start, stop):
             nc.tensor.matmul_mx(
@@ -115,127 +142,272 @@ def tile_multiheadattention_pa_kernel(tc, k, e, Wk, bk, We, be, out):
                 stop=stop,
             )
 
-        def regroup_weights(c, blk):
-            w_grouped = grouped.tile([P, PASSES, BLOCK, PACK], BF16, align_bytes=64)
-            for g in range(PASSES):
-                dst = w_grouped[:, g].rearrange("p (c i) t -> p c t i", i=4)
-                src = w_raws[c][:, g, :, blk * BLOCK : (blk + 1) * BLOCK].rearrange("p t (c i) -> p c t i", i=4)
-                if c == 0:
-                    nc.vector.tensor_copy(out=dst, in_=src)
-                else:
-                    nc.scalar.copy(out=dst, in_=src)
-            return w_grouped
+        w_grouped_of = {}
+        w_ready = {}
 
-        def transpose_tokens(tiles):
-            pairs = []
-            for first in range(0, TOKEN_TILES, 2):
-                x_grouped = grouped.tile([P, 2 * MODEL], BF16, align_bytes=64)
-                x_words = x_grouped[:].bitcast(F32).rearrange("p (j g w u) -> p j g w u", j=2, g=PASSES, u=2)
-                for j in range(2):
-                    token_words = tiles[first + j][:].bitcast(F32)
-                    flipped = psum_flip.tile([P, 2 * PASSES, P], F32, tag="flipped")
-                    for q in range(2 * PASSES):
-                        nc.tensor.transpose(flipped[:, q, :], token_words[:, q * P : (q + 1) * P], identity[:])
-                    nc.scalar.copy(out=x_words[:, j], in_=flipped[:].rearrange("p (g u) w -> p g w u", u=2))
-                pairs.append(x_grouped)
-            return pairs
+        def regroup(c, blk, g, copy):
+            if (c, blk) not in w_grouped_of:
+                w_grouped_of[(c, blk)] = grouped.tile([P, PASSES, BLOCK, PACK], BF16, name="w_grouped", align_bytes=64)
+                w_ready[(c, blk)] = new_codes(PASSES * BLOCK, "w%d%d" % (c, blk))
+            copy(
+                out=w_grouped_of[(c, blk)][:, g].rearrange("p (c i) t -> p c t i", i=4),
+                in_=w_raws[c][:, g, :, blk * BLOCK : (blk + 1) * BLOCK].rearrange("p t (c i) -> p c t i", i=4),
+            )
 
-        def project_half(x_pairs, w_block, bias_col, h_grouped, half):
-            acc = psum_acc.tile([P, TOKEN_TILES, P], F32, tag="acc")
-            for j in range(TOKEN_TILES):
+        def quantise_w_pass(c, blk, g):
+            quantise(w_ready[(c, blk)], g * BLOCK, w_grouped_of[(c, blk)][:, g].rearrange("p c t -> p (c t)"))
+
+        def quantise_w(c, blk):
+            quantise(w_ready[(c, blk)], 0, w_grouped_of[(c, blk)][:].rearrange("p g c t -> p (g c t)"))
+
+        x_grouped_of = {}
+        x_ready = {}
+
+        def transpose_tile(stream, b, j, copy=nc.scalar.copy):
+            key = (stream, b, j // 2)
+            if key not in x_grouped_of:
+                x_grouped_of[key] = grouped.tile([P, 2 * MODEL], BF16, name="x_grouped", align_bytes=64)
+                x_ready[key] = new_codes(2 * PASSES * P, "x%d%d%d" % key)
+            x_words = x_grouped_of[key][:].bitcast(F32).rearrange("p (j g w u) -> p j g w u", j=2, g=PASSES, u=2)
+            token_words = x_raws[(stream, b)][j][:].bitcast(F32)
+            flipped = psum_flip.tile([P, 2 * PASSES, P], F32, tag="flipped")
+            for q in range(2 * PASSES):
+                nc.tensor.transpose(flipped[:, q, :], token_words[:, q * P : (q + 1) * P], identity[:])
+            copy(out=x_words[:, j % 2], in_=flipped[:].rearrange("p (g u) w -> p g w u", u=2))
+
+        def quantise_x_tile(stream, b, j):
+            key = (stream, b, j // 2)
+            quantise(x_ready[key], (j % 2) * PASSES * P, x_grouped_of[key][:, (j % 2) * MODEL : (j % 2 + 1) * MODEL])
+
+        def quantise_x_pair(stream, b, n):
+            quantise(x_ready[(stream, b, n)], 0, x_grouped_of[(stream, b, n)][:])
+
+        h_grouped_of = {}
+        h_ready = {}
+
+        def new_h(step):
+            if step not in h_grouped_of:
+                h_grouped_of[step] = grouped.tile([P, BLOCK, PACK], BF16, name="h_grouped", align_bytes=64)
+                h_ready[step] = new_codes(BLOCK, "h%d%d%d" % step)
+
+        acc_of = {}
+
+        def project(step, half, tiles=range(TOKEN_TILES)):
+            c, b, blk = step
+            new_h(step)
+            if (step, half) not in acc_of:
+                acc_of[(step, half)] = psum_acc.tile([P, TOKEN_TILES, P], F32, name="acc", tag="acc")
+            acc = acc_of[(step, half)]
+            for j in tiles:
                 for g in range(PASSES):
                     mx_pass(
                         acc[:, j, :],
-                        x_pairs[j // 2],
+                        x_ready[(min(c, 1), b, j // 2)],
                         ((j % 2) * PASSES + g) * P,
-                        w_block,
+                        w_ready[(c, blk)],
                         g * BLOCK + half * P,
                         P,
                         g == 0,
                         g == PASSES - 1,
                     )
-            col = bias_col + half * P
+
+        def add_bias(step, half):
+            c, b, blk = step
+            col = c * CHUNK + blk * BLOCK + half * P
             nc.vector.tensor_tensor(
-                out=h_grouped[:, half * P : (half + 1) * P, :],
-                in0=acc[:].rearrange("p j c -> p c j"),
+                out=h_grouped_of[step][:, half * P : (half + 1) * P, :],
+                in0=acc_of[(step, half)][:].rearrange("p j c -> p c j"),
                 in1=bias[:, col : col + P].unsqueeze(2).to_broadcast([P, P, TOKEN_TILES]),
                 op=ADD,
             )
 
-        def compress(c, b, blk):
-            kc = psum_kc.tile([P, BLOCK], F32)
-            mx_pass(kc[:], h_ready[(0, b, c - 1)], blk * P, h_ready[(c, b, blk)], 0, BLOCK, True, True)
-            nc.scalar.copy(out=result[:, b, 2 * (c - 1) + blk, :], in_=kc[:])
+        h_flat_of = {}
 
-        steps = [(c, b, blk) for c in range(3) for b in range(BATCH) for blk in range(CHUNK // BLOCK)]
-        w_grouped_of = {}
-        x_grouped_of = {}
-        w_ready = {}
-        x_ready = {}
-        h_ready = {}
-
-        def start_weights(step):
+        def project_channels(step, half):
             c, b, blk = step
-            if (c, blk) not in w_grouped_of:
-                w_grouped_of[(c, blk)] = regroup_weights(c, blk)
+            new_h(step)
+            acc = psum_acc.tile([P, TOKEN_TILES, P], F32, tag="acc")
+            for j in range(TOKEN_TILES):
+                for g in range(PASSES):
+                    mx_pass(
+                        acc[:, j, :],
+                        w_ready[(c, blk)],
+                        g * BLOCK + half * P,
+                        x_ready[(min(c, 1), b, j // 2)],
+                        ((j % 2) * PASSES + g) * P,
+                        P,
+                        g == 0,
+                        g == PASSES - 1,
+                    )
+            acc_of[(step, half)] = acc
 
-        def start_tokens(step):
+        def add_channel_bias(step, half):
             c, b, blk = step
-            stream = min(c, 1)
-            if (stream, b) not in x_grouped_of:
-                x_grouped_of[(stream, b)] = transpose_tokens(x_raws[(stream, b)])
-            if b == 0 and blk == 0:
-                spread_bias(c)
+            h_flat = grouped.tile([P, SEQ], BF16, name="h_flat")
+            h_flat_of[(step, half)] = h_flat
+            i = c * (CHUNK // P) + blk * (BLOCK // P) + half
+            nc.scalar.activation(
+                out=h_flat[:].rearrange("c (u p e) -> c u p e", u=2, e=2),
+                in_=acc_of[(step, half)][:].rearrange("c (u e) p -> c u p e", e=2),
+                func=IDENTITY,
+                bias=bias_col[:, i, 0:1],
+            )
 
-        def finish(step):
-            c, b, blk = step
-            stream = min(c, 1)
-            if (c, blk) not in w_ready:
-                w_ready[(c, blk)] = quantise(
-                    w_grouped_of[(c, blk)][:].rearrange("p g c t -> p (g c t)"), "w%d%d" % (c, blk)
-                )
-            if (stream, b) not in x_ready:
-                x_ready[(stream, b)] = [
-                    quantise(pair[:], "x%d%d%d" % (stream, b, n)) for n, pair in enumerate(x_grouped_of[(stream, b)])
-                ]
-
-        for n in range(WEIGHTS_AHEAD):
-            start_weights(steps[n])
-        for n in range(TOKENS_AHEAD):
-            start_tokens(steps[n])
-        finish(steps[0])
-        finish(steps[1])
-        h_grouped_of = {}
+        def turn_half(step, half, copy):
+            flipped = psum_flip.tile([P, 2, P], F32, tag="flipped")
+            words = h_flat_of[(step, half)][:].bitcast(F32)
+            for u in range(2):
+                nc.tensor.transpose(flipped[:, u, :], words[:, u * P : (u + 1) * P], identity[:])
+            copy(
+                out=h_grouped_of[step][:, half * P : (half + 1) * P, :].bitcast(F32),
+                in_=flipped[:].rearrange("p u c -> p c u"),
+            )
 
         def quantise_h(step):
-            h_ready[step] = quantise(h_grouped_of[step][:].rearrange("p c j -> p (c j)"), "h%d%d%d" % step)
+            quantise(h_ready[step], 0, h_grouped_of[step][:].rearrange("p c j -> p (c j)"))
 
-        for n, step in enumerate(steps):
+        by_quadrant = out.rearrange("b (hg i) r d -> i r b hg d", i=HEADS_PER_PASS)
+
+        def store(b, first_hg, groups):
+            for i in range(HEADS_PER_PASS):
+                nc.sync.dma_start(
+                    out=by_quadrant[i][:, b, first_hg : first_hg + groups, :],
+                    in_=result[
+                        i * SLOTS : (i + 1) * SLOTS, b, first_hg : first_hg + groups, i * HEAD_DIM : (i + 1) * HEAD_DIM
+                    ],
+                )
+
+        def compress(step):
             c, b, blk = step
-            if n + TOKENS_AHEAD < len(steps):
-                start_tokens(steps[n + TOKENS_AHEAD])
-            if n + WEIGHTS_AHEAD < len(steps):
-                start_weights(steps[n + WEIGHTS_AHEAD])
-            h_grouped = grouped.tile([P, BLOCK, PACK], BF16, align_bytes=64)
-            h_grouped_of[step] = h_grouped
-            operands = (x_ready[(min(c, 1), b)], w_ready[(c, blk)], c * CHUNK + blk * BLOCK, h_grouped)
-            project_half(*operands, 0)
-            project_half(*operands, 1)
-            if n >= 1:
-                quantise_h(steps[n - 1])
-            if n + 2 < len(steps):
-                finish(steps[n + 2])
-            if n >= COMPRESS_LAG and steps[n - COMPRESS_LAG][0] > 0:
-                compress(*steps[n - COMPRESS_LAG])
-        quantise_h(steps[len(steps) - 1])
-        for step in steps[len(steps) - COMPRESS_LAG :]:
-            compress(*step)
+            hg = 2 * (c - 1) + blk
+            kc = psum_flip.tile([P, BLOCK], F32, tag="flipped")
+            mx_pass(kc[:], h_ready[(0, b, c - 1)], blk * P, h_ready[step], 0, BLOCK, True, True)
+            nc.scalar.copy(out=result[:, b, hg, :], in_=kc[:])
+            if b == BATCH - 1 and c == 2:
+                store(b, hg, 1)
+            elif blk == 1:
+                store(b, hg - 1, 2)
 
-        by_quadrant = out.rearrange("b (hg i) r d -> i r (b hg) d", i=HEADS_PER_PASS)
-        for i in range(HEADS_PER_PASS):
-            nc.sync.dma_start(
-                out=by_quadrant[i],
-                in_=result[i * SLOTS : (i + 1) * SLOTS].rearrange("p b hg c -> p (b hg) c")[
-                    :, :, i * HEAD_DIM : (i + 1) * HEAD_DIM
-                ],
-            )
+        vector_copy = nc.vector.tensor_copy
+        scalar_copy = nc.scalar.copy
+
+        steps = [(c, b, blk) for c in range(2) for b in range(BATCH) for blk in range(CHUNK // BLOCK)]
+        steps += [(2, b, blk) for blk in range(CHUNK // BLOCK) for b in range(BATCH)]
+        turned = ()
+
+        def mm(n):
+            if n in turned:
+                project_channels(steps[n], 1)
+                add_channel_bias(steps[n], 1)
+                project(steps[n], 0)
+                turn_half(steps[n], 1, scalar_copy)
+            else:
+                project(steps[n], 0)
+                project(steps[n], 1)
+
+        def mm_pair(n, pair):
+            project(steps[n], 0, range(2 * pair, 2 * pair + 2))
+            project(steps[n], 1, range(2 * pair, 2 * pair + 2))
+
+        def add(n):
+            add_bias(steps[n], 0)
+            if n not in turned:
+                add_bias(steps[n], 1)
+
+        def hq(n):
+            quantise_h(steps[n])
+
+        for c in range(3):
+            spread_bias(c)
+        turn_bias(4, 12)
+        regroup(0, 0, 0, vector_copy)
+        regroup(0, 1, 0, scalar_copy)
+        transpose_tile(0, 0, 0)
+        transpose_tile(0, 0, 1)
+        quantise_w_pass(0, 0, 0)
+        quantise_w_pass(0, 1, 0)
+        regroup(0, 0, 1, vector_copy)
+        quantise_x_pair(0, 0, 0)
+        regroup(0, 1, 1, scalar_copy)
+        transpose_tile(0, 0, 2)
+        transpose_tile(0, 0, 3)
+        quantise_w_pass(0, 0, 1)
+        quantise_w_pass(0, 1, 1)
+        quantise_x_tile(0, 0, 2)
+        quantise_x_tile(0, 0, 3)
+        mm_pair(0, 0)
+        transpose_tile(0, 1, 0)
+        transpose_tile(0, 1, 1)
+        mm_pair(0, 1)
+        transpose_tile(0, 1, 2)
+        transpose_tile(0, 1, 3)
+        mm(1)
+        add(0)
+        regroup(1, 0, 0, scalar_copy)
+        regroup(1, 0, 1, scalar_copy)
+        quantise_x_pair(0, 1, 0)
+        quantise_x_pair(0, 1, 1)
+        transpose_tile(1, 0, 0)
+        mm(2)
+        transpose_tile(1, 0, 1)
+        transpose_tile(1, 0, 2)
+        transpose_tile(1, 0, 3)
+        add(1)
+        hq(0)
+        quantise_w(1, 0)
+        mm(3)
+        add(2)
+        hq(1)
+        quantise_x_pair(1, 0, 0)
+        regroup(1, 1, 0, scalar_copy)
+        regroup(1, 1, 1, scalar_copy)
+        transpose_tile(1, 1, 0)
+        transpose_tile(1, 1, 1)
+        mm_pair(4, 0)
+        quantise_x_pair(1, 0, 1)
+        mm_pair(4, 1)
+        add(3)
+        hq(2)
+        transpose_tile(1, 1, 2)
+        transpose_tile(1, 1, 3)
+        quantise_w(1, 1)
+        mm(5)
+        add(4)
+        hq(3)
+        quantise_x_pair(1, 1, 0)
+        quantise_x_pair(1, 1, 1)
+        regroup(2, 0, 0, scalar_copy)
+        regroup(2, 0, 1, scalar_copy)
+        mm(6)
+        regroup(2, 1, 0, scalar_copy)
+        regroup(2, 1, 1, scalar_copy)
+        add(5)
+        hq(4)
+        mm(7)
+        add(6)
+        hq(5)
+        quantise_w(2, 0)
+        compress(steps[4])
+        mm(8)
+        add(7)
+        hq(6)
+        mm(9)
+        compress(steps[5])
+        compress(steps[6])
+        add(8)
+        hq(7)
+        quantise_w(2, 1)
+        mm(10)
+        compress(steps[7])
+        add(9)
+        hq(8)
+        mm(11)
+        compress(steps[8])
+        add(10)
+        hq(9)
+        compress(steps[9])
+        add(11)
+        hq(10)
+        compress(steps[10])
+        hq(11)
+        compress(steps[11])

@@ -53,8 +53,6 @@ def tile_multiheadattention_pa_kernel(tc, k, e, Wk, bk, We, be, out):
         nc.vector.memset(bias_rows[:].bitcast(mybir.dt.int32), 0)
         ones = const.tile([P, P], BF16)
         nc.vector.memset(ones[:], 1.0)
-        nc.scalar.dma_start(out=bias_rows[0:1, 0:CHUNK], in_=be.rearrange("(o c) -> o c", o=1))
-        nc.scalar.dma_start(out=bias_rows[0:1, CHUNK:bias_cols], in_=bk.rearrange("(o c) -> o c", o=1))
         nc.scalar.copy(out=scratch[:], in_=ones[:, 0:2])
 
         def load_weight_pass(w, w_raw, g, col0):
@@ -84,6 +82,8 @@ def tile_multiheadattention_pa_kernel(tc, k, e, Wk, bk, We, be, out):
                     raw.tile([P, MODEL], BF16, name="x_raw%d%d%d" % (stream, b, j)) for j in range(TOKEN_TILES)
                 ]
         load_weight_pass(We, w_raws[0], 0, 0)
+        nc.sync.dma_start(out=bias_rows[0:1, 0:CHUNK], in_=be.rearrange("(o c) -> o c", o=1))
+        nc.sync.dma_start(out=bias_rows[0:1, CHUNK:bias_cols], in_=bk.rearrange("(o c) -> o c", o=1))
         load_token_tiles(e, 0, x_raws[(0, 0)], (0, 1))
         load_weight_pass(We, w_raws[0], 1, 0)
         load_token_tiles(e, 0, x_raws[(0, 0)], (2, 3))
@@ -317,9 +317,6 @@ def tile_multiheadattention_pa_kernel(tc, k, e, Wk, bk, We, be, out):
         def hq(n):
             quantise_h(steps[n])
 
-        for c in range(3):
-            spread_bias(c)
-        turn_bias(4, 12)
         regroup(0, 0, 0, vector_copy)
         regroup(0, 1, 0, scalar_copy)
         transpose_tile(0, 0, 0)
@@ -331,16 +328,19 @@ def tile_multiheadattention_pa_kernel(tc, k, e, Wk, bk, We, be, out):
         regroup(0, 1, 1, scalar_copy)
         transpose_tile(0, 0, 2)
         transpose_tile(0, 0, 3)
+        spread_bias(0)
         quantise_w_pass(0, 0, 1)
         quantise_w_pass(0, 1, 1)
         quantise_x_tile(0, 0, 2)
         quantise_x_tile(0, 0, 3)
-        mm_pair(0, 0)
         transpose_tile(0, 1, 0)
-        transpose_tile(0, 1, 1)
+        mm_pair(0, 0)
         mm_pair(0, 1)
+        transpose_tile(0, 1, 1)
         transpose_tile(0, 1, 2)
         transpose_tile(0, 1, 3)
+        spread_bias(1)
+        spread_bias(2)
         mm(1)
         add(0)
         regroup(1, 0, 0, scalar_copy)
@@ -354,9 +354,9 @@ def tile_multiheadattention_pa_kernel(tc, k, e, Wk, bk, We, be, out):
         transpose_tile(1, 0, 3)
         add(1)
         hq(0)
-        quantise_w(1, 0)
         mm(3)
         add(2)
+        quantise_w(1, 0)
         hq(1)
         quantise_x_pair(1, 0, 0)
         regroup(1, 1, 0, scalar_copy)

@@ -263,19 +263,32 @@ def tile_multiheadattention_pa_kernel(tc, k, e, Wk, bk, We, be, out):
                 in_=flipped[:].rearrange("p u c -> p c u"),
             )
 
+        def add_bias_gpsimd(step, half):
+            c, b, blk = step
+            col = c * CHUNK + blk * BLOCK + half * P
+            h_sum = grouped.tile([P, P, TOKEN_TILES], F32, name="h_sum")
+            nc.scalar.copy(out=h_sum[:], in_=acc_of[(step, half)][:].rearrange("p j c -> p c j"))
+            nc.gpsimd.tensor_tensor(
+                out=h_grouped_of[step][:, half * P : (half + 1) * P, :],
+                in0=h_sum[:],
+                in1=bias[:, col : col + P].unsqueeze(2).to_broadcast([P, P, TOKEN_TILES]),
+                op=ADD,
+            )
+
         def quantise_h(step):
             quantise(h_ready[step], 0, h_grouped_of[step][:].rearrange("p c j -> p (c j)"))
 
         by_quadrant = out.rearrange("b (hg i) r d -> i r b hg d", i=HEADS_PER_PASS)
 
-        def store(b, first_hg, groups):
-            for i in range(HEADS_PER_PASS):
-                nc.sync.dma_start(
-                    out=by_quadrant[i][:, b, first_hg : first_hg + groups, :],
-                    in_=result[
-                        i * SLOTS : (i + 1) * SLOTS, b, first_hg : first_hg + groups, i * HEAD_DIM : (i + 1) * HEAD_DIM
-                    ],
-                )
+        def store(first_hg, groups, heads=range(HEADS_PER_PASS)):
+            for i in heads:
+                for hg in range(first_hg, first_hg + groups):
+                    nc.sync.dma_start(
+                        out=by_quadrant[i][:, :, hg, :],
+                        in_=result[i * SLOTS : (i + 1) * SLOTS, :, hg, i * HEAD_DIM : (i + 1) * HEAD_DIM],
+                    )
+
+        store_after = {(1, 1, 1): (0, 2), (2, 1, 0): (2, 1), (2, 1, 1): (3, 1)}
 
         def compress(step):
             c, b, blk = step
@@ -283,26 +296,38 @@ def tile_multiheadattention_pa_kernel(tc, k, e, Wk, bk, We, be, out):
             kc = psum_flip.tile([P, BLOCK], F32, tag="flipped")
             mx_pass(kc[:], h_ready[(0, b, c - 1)], blk * P, h_ready[step], 0, BLOCK, True, True)
             nc.scalar.copy(out=result[:, b, hg, :], in_=kc[:])
-            if b == BATCH - 1 and c == 2:
-                store(b, hg, 1)
-            elif blk == 1:
-                store(b, hg - 1, 2)
+            if step in store_after:
+                store(*store_after[step])
+
+        def quantise_h_half(step, half):
+            quantise(
+                h_ready[step], half * P, h_grouped_of[step][:, half * P : (half + 1) * P, :].rearrange("p c j -> p (c j)")
+            )
+
+        def compress_half(step, half):
+            c, b, blk = step
+            hg = 2 * (c - 1) + blk
+            kc = psum_flip.tile([P, P], F32, tag="flipped")
+            mx_pass(kc[:], h_ready[(0, b, c - 1)], blk * P, h_ready[step], half * P, P, True, True)
+            nc.scalar.copy(out=result[:, b, hg, half * P : (half + 1) * P], in_=kc[:])
+            store(hg, 1, (2 * half, 2 * half + 1))
 
         vector_copy = nc.vector.tensor_copy
         scalar_copy = nc.scalar.copy
 
         steps = [(c, b, blk) for c in range(2) for b in range(BATCH) for blk in range(CHUNK // BLOCK)]
         steps += [(2, b, blk) for blk in range(CHUNK // BLOCK) for b in range(BATCH)]
-        turned = ()
+        turned = (6, 8, 10)
 
         def mm(n):
             if n in turned:
                 project_channels(steps[n], 1)
                 add_channel_bias(steps[n], 1)
                 project(steps[n], 0)
-                turn_half(steps[n], 1, scalar_copy)
             else:
                 project(steps[n], 0)
+                if n - 1 in turned:
+                    turn_half(steps[n - 1], 1, scalar_copy)
                 project(steps[n], 1)
 
         def mm_pair(n, pair):
@@ -341,19 +366,20 @@ def tile_multiheadattention_pa_kernel(tc, k, e, Wk, bk, We, be, out):
         transpose_tile(0, 1, 3)
         spread_bias(1)
         spread_bias(2)
+        turn_bias(4, 12)
         mm(1)
         add(0)
         regroup(1, 0, 0, scalar_copy)
-        regroup(1, 0, 1, scalar_copy)
         quantise_x_pair(0, 1, 0)
         quantise_x_pair(0, 1, 1)
         transpose_tile(1, 0, 0)
-        mm(2)
         transpose_tile(1, 0, 1)
+        mm(2)
         transpose_tile(1, 0, 2)
         transpose_tile(1, 0, 3)
         add(1)
         hq(0)
+        regroup(1, 0, 1, vector_copy)
         mm(3)
         add(2)
         quantise_w(1, 0)
@@ -406,8 +432,11 @@ def tile_multiheadattention_pa_kernel(tc, k, e, Wk, bk, We, be, out):
         add(10)
         hq(9)
         compress(steps[9])
-        add(11)
+        add_bias(steps[11], 0)
         hq(10)
+        add_bias(steps[11], 1)
         compress(steps[10])
-        hq(11)
-        compress(steps[11])
+        quantise_h_half(steps[11], 0)
+        quantise_h_half(steps[11], 1)
+        compress_half(steps[11], 0)
+        compress_half(steps[11], 1)

@@ -342,44 +342,48 @@ def tile_multiheadattention_pa_kernel(tc, k, e, Wk, bk, We, be, out):
         def hq(n):
             quantise_h(steps[n])
 
+        warm = psum_flip.tile([P, 2 * PASSES, P], F32, tag="flipped")
+        for i in range(16):
+            nc.tensor.transpose(warm[:, i % 4, :], identity[:], identity[:])
         regroup(0, 0, 0, vector_copy)
-        regroup(0, 1, 0, scalar_copy)
+        regroup(0, 1, 0, vector_copy)
         transpose_tile(0, 0, 0)
         transpose_tile(0, 0, 1)
+        spread_bias(0)
+        spread_bias(1)
+        spread_bias(2)
+        turn_bias(4, 12)
         quantise_w_pass(0, 0, 0)
         quantise_w_pass(0, 1, 0)
         regroup(0, 0, 1, vector_copy)
         quantise_x_pair(0, 0, 0)
-        regroup(0, 1, 1, scalar_copy)
+        quantise_w_pass(0, 0, 1)
         transpose_tile(0, 0, 2)
         transpose_tile(0, 0, 3)
-        spread_bias(0)
-        quantise_w_pass(0, 0, 1)
-        quantise_w_pass(0, 1, 1)
         quantise_x_tile(0, 0, 2)
         quantise_x_tile(0, 0, 3)
+        regroup(0, 1, 1, vector_copy)
         transpose_tile(0, 1, 0)
-        mm_pair(0, 0)
-        mm_pair(0, 1)
+        mm(0)
+
         transpose_tile(0, 1, 1)
         transpose_tile(0, 1, 2)
         transpose_tile(0, 1, 3)
-        spread_bias(1)
-        spread_bias(2)
-        turn_bias(4, 12)
-        mm(1)
         add(0)
+        quantise_w_pass(0, 1, 1)
+        mm(1)
         regroup(1, 0, 0, scalar_copy)
         quantise_x_pair(0, 1, 0)
+        add_bias(steps[1], 0)
         quantise_x_pair(0, 1, 1)
+        add_bias(steps[1], 1)
+        hq(0)
+        regroup(1, 0, 1, scalar_copy)
         transpose_tile(1, 0, 0)
-        transpose_tile(1, 0, 1)
         mm(2)
+        transpose_tile(1, 0, 1)
         transpose_tile(1, 0, 2)
         transpose_tile(1, 0, 3)
-        add(1)
-        hq(0)
-        regroup(1, 0, 1, vector_copy)
         mm(3)
         add(2)
         quantise_w(1, 0)

@@ -37,7 +37,7 @@ FLOPS = 2 * BATCH * SEQ * MODEL * HEADS * (HEAD_DIM + SLOTS) + 2 * BATCH * HEADS
 def tile_multiheadattention_pa_kernel(tc, k, e, Wk, bk, We, be, out):
     nc = tc.nc
     with ExitStack() as ctx:
-        ctx.enter_context(tc.manual_schedule())
+        ctx.enter_context(tc.manual_schedule(engines={mybir.EngineType.DVE, mybir.EngineType.Activation, mybir.EngineType.SP}))
         const = ctx.enter_context(tc.tile_pool(name="const", bufs=1))
         raw = ctx.enter_context(tc.tile_pool(name="raw", bufs=1))
         grouped = ctx.enter_context(tc.tile_pool(name="grouped", bufs=4))
@@ -82,9 +82,9 @@ def tile_multiheadattention_pa_kernel(tc, k, e, Wk, bk, We, be, out):
                     raw.tile([P, MODEL], BF16, name="x_raw%d%d%d" % (stream, b, j)) for j in range(TOKEN_TILES)
                 ]
         load_weight_pass(We, w_raws[0], 0, 0)
+        load_token_tiles(e, 0, x_raws[(0, 0)], (0, 1))
         nc.sync.dma_start(out=bias_rows[0:1, 0:CHUNK], in_=be.rearrange("(o c) -> o c", o=1))
         nc.sync.dma_start(out=bias_rows[0:1, CHUNK:bias_cols], in_=bk.rearrange("(o c) -> o c", o=1))
-        load_token_tiles(e, 0, x_raws[(0, 0)], (0, 1))
         load_weight_pass(We, w_raws[0], 1, 0)
         load_token_tiles(e, 0, x_raws[(0, 0)], (2, 3))
         load_token_tiles(e, 1, x_raws[(0, 1)], range(TOKEN_TILES))
@@ -104,17 +104,20 @@ def tile_multiheadattention_pa_kernel(tc, k, e, Wk, bk, We, be, out):
 
         bias_col = const.tile([P, bias_cols // P, 2], F32)
 
-        def turn_bias(first, last):
-            turned = psum_flip.tile([P, last - first, 2], F32, tag="flipped")
-            for i in range(first, last):
+        bias_col_of = {}
+
+        def turn_bias(blocks):
+            columns = psum_flip.tile([P, len(blocks), 2], F32, tag="flipped")
+            for n, i in enumerate(blocks):
                 nc.tensor.matmul(
-                    out=turned[:, i - first, :],
+                    out=columns[:, n, :],
                     lhsT=bias_rows[:, i * P : (i + 1) * P],
                     rhs=ones[:, 0:2],
                     start=True,
                     stop=True,
                 )
-            nc.scalar.copy(out=bias_col[:, first:last, :], in_=turned[:])
+                bias_col_of[i] = bias_col[:, n, 0:1]
+            nc.scalar.copy(out=bias_col[:, 0 : len(blocks), :], in_=columns[:])
 
         result = const.tile([P, BATCH, HEADS // HEADS_PER_PASS, BLOCK], F32)
 
@@ -168,7 +171,10 @@ def tile_multiheadattention_pa_kernel(tc, k, e, Wk, bk, We, be, out):
             if key not in x_grouped_of:
                 x_grouped_of[key] = grouped.tile([P, 2 * MODEL], BF16, name="x_grouped", align_bytes=64)
                 x_ready[key] = new_codes(2 * PASSES * P, "x%d%d%d" % key)
-            x_words = x_grouped_of[key][:].bitcast(F32).rearrange("p (j g w u) -> p j g w u", j=2, g=PASSES, u=2)
+            if stream == 0:
+                x_words = x_grouped_of[key][:].bitcast(F32).rearrange("p (j g w u) -> p j g w u", j=2, g=PASSES, u=2)
+            else:
+                x_words = x_grouped_of[key][:].bitcast(F32).rearrange("p (g j w u) -> p j g w u", j=2, g=PASSES, u=2)
             token_words = x_raws[(stream, b)][j][:].bitcast(F32)
             flipped = psum_flip.tile([P, 2 * PASSES, P], F32, tag="flipped")
             for q in range(2 * PASSES):
@@ -185,12 +191,34 @@ def tile_multiheadattention_pa_kernel(tc, k, e, Wk, bk, We, be, out):
         h_grouped_of = {}
         h_ready = {}
 
+        joint_of = {}
+
         def new_h(step):
-            if step not in h_grouped_of:
-                h_grouped_of[step] = grouped.tile([P, BLOCK, PACK], BF16, name="h_grouped", align_bytes=64)
+            c, b, blk = step
+            if step in h_grouped_of:
+                return
+            if c < 0:
+                if (c, b) not in joint_of:
+                    h_joint = grouped.tile([P, 2 * BLOCK, PACK], BF16, name="h_joint", align_bytes=64)
+                    joint_of[(c, b)] = (h_joint, new_codes(2 * BLOCK, "h%d%d" % (c, b)))
+                values, (codes, scales) = joint_of[(c, b)]
+                own = slice(blk * BLOCK, (blk + 1) * BLOCK)
+                h_grouped_of[step] = values[:, own, :]
+                h_ready[step] = (codes[:, own], scales[:, own])
+            else:
+                values = grouped.tile([P, BLOCK, PACK], BF16, name="h_grouped", align_bytes=64)
+                h_grouped_of[step] = values[:]
                 h_ready[step] = new_codes(BLOCK, "h%d%d%d" % step)
 
+        def quantise_joint(c, b):
+            values, target = joint_of[(c, b)]
+            quantise(target, 0, values[:].rearrange("p c j -> p (c j)"))
+
+
         acc_of = {}
+
+        def x_column(stream, j, g):
+            return ((j % 2) * PASSES + g if stream == 0 else g * 2 + j % 2) * P
 
         def project(step, half, tiles=range(TOKEN_TILES)):
             c, b, blk = step
@@ -203,7 +231,7 @@ def tile_multiheadattention_pa_kernel(tc, k, e, Wk, bk, We, be, out):
                     mx_pass(
                         acc[:, j, :],
                         x_ready[(min(c, 1), b, j // 2)],
-                        ((j % 2) * PASSES + g) * P,
+                        x_column(min(c, 1), j, g),
                         w_ready[(c, blk)],
                         g * BLOCK + half * P,
                         P,
@@ -223,23 +251,24 @@ def tile_multiheadattention_pa_kernel(tc, k, e, Wk, bk, We, be, out):
 
         h_flat_of = {}
 
-        def project_channels(step, half):
+        def project_channels(step, half, tiles=range(2)):
             c, b, blk = step
             new_h(step)
-            acc = psum_acc.tile([P, TOKEN_TILES, P], F32, tag="acc")
-            for j in range(TOKEN_TILES):
+            if (step, half) not in acc_of:
+                acc_of[(step, half)] = psum_acc.tile([P, TOKEN_TILES, P], F32, name="acc", tag="acc")
+            acc = acc_of[(step, half)]
+            for pair in tiles:
                 for g in range(PASSES):
                     mx_pass(
-                        acc[:, j, :],
+                        acc[:, 2 * pair : 2 * pair + 2, :].rearrange("c j p -> c (j p)"),
                         w_ready[(c, blk)],
                         g * BLOCK + half * P,
-                        x_ready[(min(c, 1), b, j // 2)],
-                        ((j % 2) * PASSES + g) * P,
-                        P,
+                        x_ready[(1, b, pair)],
+                        g * 2 * P,
+                        2 * P,
                         g == 0,
                         g == PASSES - 1,
                     )
-            acc_of[(step, half)] = acc
 
         def add_channel_bias(step, half):
             c, b, blk = step
@@ -250,7 +279,7 @@ def tile_multiheadattention_pa_kernel(tc, k, e, Wk, bk, We, be, out):
                 out=h_flat[:].rearrange("c (u p e) -> c u p e", u=2, e=2),
                 in_=acc_of[(step, half)][:].rearrange("c (u e) p -> c u p e", e=2),
                 func=IDENTITY,
-                bias=bias_col[:, i, 0:1],
+                bias=bias_col_of[i],
             )
 
         def turn_half(step, half, copy):
@@ -276,7 +305,7 @@ def tile_multiheadattention_pa_kernel(tc, k, e, Wk, bk, We, be, out):
             )
 
         def quantise_h(step):
-            quantise(h_ready[step], 0, h_grouped_of[step][:].rearrange("p c j -> p (c j)"))
+            quantise(h_ready[step], 0, h_grouped_of[step].rearrange("p c j -> p (c j)"))
 
         by_quadrant = out.rearrange("b (hg i) r d -> i r b hg d", i=HEADS_PER_PASS)
 
@@ -317,27 +346,39 @@ def tile_multiheadattention_pa_kernel(tc, k, e, Wk, bk, We, be, out):
 
         steps = [(c, b, blk) for c in range(2) for b in range(BATCH) for blk in range(CHUNK // BLOCK)]
         steps += [(2, b, blk) for blk in range(CHUNK // BLOCK) for b in range(BATCH)]
-        turned = (6, 8, 10)
+        turned = {6: (1,), 8: (1,), 10: (1,)}
 
         def mm(n):
-            if n in turned:
-                project_channels(steps[n], 1)
-                add_channel_bias(steps[n], 1)
-                project(steps[n], 0)
-            else:
-                project(steps[n], 0)
-                if n - 1 in turned:
-                    turn_half(steps[n - 1], 1, scalar_copy)
-                project(steps[n], 1)
+            halves = turned.get(n, ())
+            for half in halves:
+                project_channels(steps[n], half)
+                add_channel_bias(steps[n], half)
+            rest = [half for half in range(2) if half not in halves]
+            for i, half in enumerate(rest):
+                project(steps[n], half)
+                if i == 0:
+                    turn(n - 1)
+            if not rest:
+                turn(n - 1)
+
+        def turn(n):
+            for half in turned.get(n, ()):
+                turn_half(steps[n], half, scalar_copy)
 
         def mm_pair(n, pair):
-            project(steps[n], 0, range(2 * pair, 2 * pair + 2))
-            project(steps[n], 1, range(2 * pair, 2 * pair + 2))
+            tiles = range(2 * pair, 2 * pair + 2)
+            for half in range(2):
+                if half in turned.get(n, ()):
+                    project_channels(steps[n], half, tiles)
+                    if pair == 1:
+                        add_channel_bias(steps[n], half)
+                else:
+                    project(steps[n], half, tiles)
 
         def add(n):
-            add_bias(steps[n], 0)
-            if n not in turned:
-                add_bias(steps[n], 1)
+            for half in range(2):
+                if half not in turned.get(n, ()):
+                    add_bias(steps[n], half)
 
         def hq(n):
             quantise_h(steps[n])
@@ -352,7 +393,12 @@ def tile_multiheadattention_pa_kernel(tc, k, e, Wk, bk, We, be, out):
         spread_bias(0)
         spread_bias(1)
         spread_bias(2)
-        turn_bias(4, 12)
+        turn_bias(
+            [
+                c * (CHUNK // P) + blk * (BLOCK // P) + half
+                for c, blk, half in sorted({(steps[n][0], steps[n][2], half) for n in turned for half in turned[n]})
+            ]
+        )
         quantise_w_pass(0, 0, 0)
         quantise_w_pass(0, 1, 0)
         regroup(0, 0, 1, vector_copy)
@@ -365,7 +411,6 @@ def tile_multiheadattention_pa_kernel(tc, k, e, Wk, bk, We, be, out):
         regroup(0, 1, 1, vector_copy)
         transpose_tile(0, 1, 0)
         mm(0)
-
         transpose_tile(0, 1, 1)
         transpose_tile(0, 1, 2)
         transpose_tile(0, 1, 3)

@@ -153,8 +153,8 @@ def tile_multiheadattention_pa_kernel(tc, k, e, Wk, bk, We, be, out):
                 w_grouped_of[(c, blk)] = grouped.tile([P, PASSES, BLOCK, PACK], BF16, name="w_grouped", align_bytes=64)
                 w_ready[(c, blk)] = new_codes(PASSES * BLOCK, "w%d%d" % (c, blk))
             copy(
-                out=w_grouped_of[(c, blk)][:, g].rearrange("p (c i) t -> p c t i", i=4),
-                in_=w_raws[c][:, g, :, blk * BLOCK : (blk + 1) * BLOCK].rearrange("p t (c i) -> p c t i", i=4),
+                out=w_grouped_of[(c, blk)][:, g].rearrange("p (c i) t -> p c t i", i=8),
+                in_=w_raws[c][:, g, :, blk * BLOCK : (blk + 1) * BLOCK].rearrange("p t (c i) -> p c t i", i=8),
             )
 
         def quantise_w_pass(c, blk, g):

from contextlib import ExitStack

import concourse.mybir as mybir
from concourse.masks import make_identity

BF16 = mybir.dt.bfloat16
F32 = mybir.dt.float32
U32 = mybir.dt.uint32
U8 = mybir.dt.uint8
FP8X4 = mybir.dt.float8_e4m3fn_x4
ADD = mybir.AluOpType.add
IDENTITY = mybir.ActivationFunctionType.Identity

BATCH = 2
SEQ = 512
MODEL = 1024
HEADS = 16
HEAD_DIM = 64
SLOTS = 32

P = 128
PACK = 4
K_PASS = P * PACK
PASSES = MODEL // K_PASS
TOKEN_TILES = SEQ // P
CHUNK = 512
BLOCK = 256
HEADS_PER_PASS = P // SLOTS

TOKENS_AHEAD = 2
WEIGHTS_AHEAD = 3
COMPRESS_LAG = 3

FLOPS = 2 * BATCH * SEQ * MODEL * HEADS * (HEAD_DIM + SLOTS) + 2 * BATCH * HEADS * SLOTS * HEAD_DIM * SEQ


def tile_multiheadattention_pa_kernel(tc, k, e, Wk, bk, We, be, out):
    nc = tc.nc
    with ExitStack() as ctx:
        ctx.enter_context(tc.manual_schedule(engines={mybir.EngineType.DVE, mybir.EngineType.Activation, mybir.EngineType.SP}))
        const = ctx.enter_context(tc.tile_pool(name="const", bufs=1))
        raw = ctx.enter_context(tc.tile_pool(name="raw", bufs=1))
        grouped = ctx.enter_context(tc.tile_pool(name="grouped", bufs=4))
        quantised = ctx.enter_context(tc.tile_pool(name="quantised", bufs=1))
        psum_flip = ctx.enter_context(tc.psum_pool(name="psum_flip", bufs=4))
        psum_acc = ctx.enter_context(tc.psum_pool(name="psum_acc", bufs=4))

        identity = const.tile([P, P], F32)
        make_identity(nc, identity[:])
        scratch = const.tile([P, 2], BF16)
        bias_cols = 3 * CHUNK
        bias_rows = const.tile([P, bias_cols], BF16)
        nc.vector.memset(bias_rows[:].bitcast(mybir.dt.int32), 0)
        ones = const.tile([P, P], BF16)
        nc.vector.memset(ones[:], 1.0)
        nc.scalar.copy(out=scratch[:], in_=ones[:, 0:2])

        def load_weight_pass(w, w_raw, g, col0):
            for u in range(2):
                row0 = K_PASS * g + 2 * P * u
                nc.sync.dma_start(
                    out=w_raw[:, g, 2 * u : 2 * u + 2, :],
                    in_=w[row0 : row0 + 2 * P, col0 : col0 + CHUNK].rearrange("(q e) c -> q e c", e=2),
                )

        def load_weight_chunk(w, w_raw, col0):
            for g in range(PASSES):
                load_weight_pass(w, w_raw, g, col0)

        def load_token_tiles(x, b, tiles, js):
            by_tile = x[b].rearrange("(p j) d -> j p d", j=TOKEN_TILES)
            for j in js:
                nc.sync.dma_start(out=tiles[j][:], in_=by_tile[j])

        w_raws = {}
        x_raws = {}
        for c in range(3):
            w_raws[c] = raw.tile([P, PASSES, PACK, CHUNK], BF16, name="w_raw%d" % c)
        for stream in range(2):
            for b in range(BATCH):
                x_raws[(stream, b)] = [
                    raw.tile([P, MODEL], BF16, name="x_raw%d%d%d" % (stream, b, j)) for j in range(TOKEN_TILES)
                ]
        load_weight_pass(We, w_raws[0], 0, 0)
        load_token_tiles(e, 0, x_raws[(0, 0)], (0, 1))
        nc.sync.dma_start(out=bias_rows[0:1, 0:CHUNK], in_=be.rearrange("(o c) -> o c", o=1))
        nc.sync.dma_start(out=bias_rows[0:1, CHUNK:bias_cols], in_=bk.rearrange("(o c) -> o c", o=1))
        load_weight_pass(We, w_raws[0], 1, 0)
        load_token_tiles(e, 0, x_raws[(0, 0)], (2, 3))
        load_token_tiles(e, 1, x_raws[(0, 1)], range(TOKEN_TILES))
        load_weight_chunk(Wk, w_raws[1], 0)
        load_token_tiles(k, 0, x_raws[(1, 0)], range(TOKEN_TILES))
        load_token_tiles(k, 1, x_raws[(1, 1)], range(TOKEN_TILES))
        load_weight_chunk(Wk, w_raws[2], CHUNK)

        bias = const.tile([P, bias_cols], BF16)

        def spread_bias(c):
            spread = psum_flip.tile([P, CHUNK], BF16, tag="flipped")
            nc.tensor.matmul(
                out=spread[:], lhsT=ones[:], rhs=bias_rows[:, c * CHUNK : (c + 1) * CHUNK], start=True, stop=True
            )
            nc.scalar.copy(out=bias[:, c * CHUNK : (c + 1) * CHUNK], in_=spread[:])

        bias_col = const.tile([P, bias_cols // P, 2], F32)

        bias_col_of = {}

        def turn_bias(blocks):
            columns = psum_flip.tile([P, len(blocks), 2], F32, tag="flipped")
            for n, i in enumerate(blocks):
                nc.tensor.matmul(
                    out=columns[:, n, :],
                    lhsT=bias_rows[:, i * P : (i + 1) * P],
                    rhs=ones[:, 0:2],
                    start=True,
                    stop=True,
                )
                bias_col_of[i] = bias_col[:, n, 0:1]
            nc.scalar.copy(out=bias_col[:, 0 : len(blocks), :], in_=columns[:])

        result = const.tile([P, BATCH, HEADS // HEADS_PER_PASS, BLOCK], F32)

        def new_codes(words, name):
            codes = quantised.tile([P, words], U32, name=name + "_codes", align_bytes=64)
            scales = quantised.tile([P, words], U8, name=name + "_scales", align_bytes=64)
            return codes, scales

        def quantise(target, first, values):
            words = values.shape[1] // PACK
            nc.vector.quantize_mx(
                out=target[0][:, first : first + words].bitcast(FP8X4),
                scales=target[1][:, first : first + words],
                in_=values,
            )

        def mx_pass(acc, stationary, s_col, moving, m_col, width, start, stop):
            nc.tensor.matmul_mx(
                out=acc,
                lhsT=stationary[0][:, s_col : s_col + P].bitcast(FP8X4),
                lhsT_scale=stationary[1][:, s_col : s_col + P],
                rhs=moving[0][:, m_col : m_col + width].bitcast(FP8X4),
                rhs_scale=moving[1][:, m_col : m_col + width],
                start=start,
                stop=stop,
            )

        w_grouped_of = {}
        w_ready = {}

        def regroup(c, blk, g, copy):
            if (c, blk) not in w_grouped_of:
                w_grouped_of[(c, blk)] = grouped.tile([P, PASSES, BLOCK, PACK], BF16, name="w_grouped", align_bytes=64)
                w_ready[(c, blk)] = new_codes(PASSES * BLOCK, "w%d%d" % (c, blk))
            copy(
                out=w_grouped_of[(c, blk)][:, g].rearrange("p (c i) t -> p c t i", i=8),
                in_=w_raws[c][:, g, :, blk * BLOCK : (blk + 1) * BLOCK].rearrange("p t (c i) -> p c t i", i=8),
            )

        def quantise_w_pass(c, blk, g):
            quantise(w_ready[(c, blk)], g * BLOCK, w_grouped_of[(c, blk)][:, g].rearrange("p c t -> p (c t)"))

        def quantise_w(c, blk):
            quantise(w_ready[(c, blk)], 0, w_grouped_of[(c, blk)][:].rearrange("p g c t -> p (g c t)"))

        x_grouped_of = {}
        x_ready = {}

        def transpose_tile(stream, b, j, copy=nc.scalar.copy):
            key = (stream, b, j // 2)
            if key not in x_grouped_of:
                x_grouped_of[key] = grouped.tile([P, 2 * MODEL], BF16, name="x_grouped", align_bytes=64)
                x_ready[key] = new_codes(2 * PASSES * P, "x%d%d%d" % key)
            if stream == 0:
                x_words = x_grouped_of[key][:].bitcast(F32).rearrange("p (j g w u) -> p j g w u", j=2, g=PASSES, u=2)
            else:
                x_words = x_grouped_of[key][:].bitcast(F32).rearrange("p (g j w u) -> p j g w u", j=2, g=PASSES, u=2)
            token_words = x_raws[(stream, b)][j][:].bitcast(F32)
            flipped = psum_flip.tile([P, 2 * PASSES, P], F32, tag="flipped")
            for q in range(2 * PASSES):
                nc.tensor.transpose(flipped[:, q, :], token_words[:, q * P : (q + 1) * P], identity[:])
            copy(out=x_words[:, j % 2], in_=flipped[:].rearrange("p (g u) w -> p g w u", u=2))

        def quantise_x_tile(stream, b, j):
            key = (stream, b, j // 2)
            quantise(x_ready[key], (j % 2) * PASSES * P, x_grouped_of[key][:, (j % 2) * MODEL : (j % 2 + 1) * MODEL])

        def quantise_x_pair(stream, b, n):
            quantise(x_ready[(stream, b, n)], 0, x_grouped_of[(stream, b, n)][:])

        h_grouped_of = {}
        h_ready = {}

        joint_of = {}

        def new_h(step):
            c, b, blk = step
            if step in h_grouped_of:
                return
            if c < 0:
                if (c, b) not in joint_of:
                    h_joint = grouped.tile([P, 2 * BLOCK, PACK], BF16, name="h_joint", align_bytes=64)
                    joint_of[(c, b)] = (h_joint, new_codes(2 * BLOCK, "h%d%d" % (c, b)))
                values, (codes, scales) = joint_of[(c, b)]
                own = slice(blk * BLOCK, (blk + 1) * BLOCK)
                h_grouped_of[step] = values[:, own, :]
                h_ready[step] = (codes[:, own], scales[:, own])
            else:
                values = grouped.tile([P, BLOCK, PACK], BF16, name="h_grouped", align_bytes=64)
                h_grouped_of[step] = values[:]
                h_ready[step] = new_codes(BLOCK, "h%d%d%d" % step)

        def quantise_joint(c, b):
            values, target = joint_of[(c, b)]
            quantise(target, 0, values[:].rearrange("p c j -> p (c j)"))


        acc_of = {}

        def x_column(stream, j, g):
            return ((j % 2) * PASSES + g if stream == 0 else g * 2 + j % 2) * P

        def project(step, half, tiles=range(TOKEN_TILES)):
            c, b, blk = step
            new_h(step)
            if (step, half) not in acc_of:
                acc_of[(step, half)] = psum_acc.tile([P, TOKEN_TILES, P], F32, name="acc", tag="acc")
            acc = acc_of[(step, half)]
            for j in tiles:
                for g in range(PASSES):
                    mx_pass(
                        acc[:, j, :],
                        x_ready[(min(c, 1), b, j // 2)],
                        x_column(min(c, 1), j, g),
                        w_ready[(c, blk)],
                        g * BLOCK + half * P,
                        P,
                        g == 0,
                        g == PASSES - 1,
                    )

        def add_bias(step, half):
            c, b, blk = step
            col = c * CHUNK + blk * BLOCK + half * P
            nc.vector.tensor_tensor(
                out=h_grouped_of[step][:, half * P : (half + 1) * P, :],
                in0=acc_of[(step, half)][:].rearrange("p j c -> p c j"),
                in1=bias[:, col : col + P].unsqueeze(2).to_broadcast([P, P, TOKEN_TILES]),
                op=ADD,
            )

        h_flat_of = {}

        def project_channels(step, half, tiles=range(2)):
            c, b, blk = step
            new_h(step)
            if (step, half) not in acc_of:
                acc_of[(step, half)] = psum_acc.tile([P, TOKEN_TILES, P], F32, name="acc", tag="acc")
            acc = acc_of[(step, half)]
            for pair in tiles:
                for g in range(PASSES):
                    mx_pass(
                        acc[:, 2 * pair : 2 * pair + 2, :].rearrange("c j p -> c (j p)"),
                        w_ready[(c, blk)],
                        g * BLOCK + half * P,
                        x_ready[(1, b, pair)],
                        g * 2 * P,
                        2 * P,
                        g == 0,
                        g == PASSES - 1,
                    )

        def add_channel_bias(step, half):
            c, b, blk = step
            h_flat = grouped.tile([P, SEQ], BF16, name="h_flat")
            h_flat_of[(step, half)] = h_flat
            i = c * (CHUNK // P) + blk * (BLOCK // P) + half
            nc.scalar.activation(
                out=h_flat[:].rearrange("c (u p e) -> c u p e", u=2, e=2),
                in_=acc_of[(step, half)][:].rearrange("c (u e) p -> c u p e", e=2),
                func=IDENTITY,
                bias=bias_col_of[i],
            )

        def turn_half(step, half, copy):
            flipped = psum_flip.tile([P, 2, P], F32, tag="flipped")
            words = h_flat_of[(step, half)][:].bitcast(F32)
            for u in range(2):
                nc.tensor.transpose(flipped[:, u, :], words[:, u * P : (u + 1) * P], identity[:])
            copy(
                out=h_grouped_of[step][:, half * P : (half + 1) * P, :].bitcast(F32),
                in_=flipped[:].rearrange("p u c -> p c u"),
            )

        def add_bias_gpsimd(step, half):
            c, b, blk = step
            col = c * CHUNK + blk * BLOCK + half * P
            h_sum = grouped.tile([P, P, TOKEN_TILES], F32, name="h_sum")
            nc.scalar.copy(out=h_sum[:], in_=acc_of[(step, half)][:].rearrange("p j c -> p c j"))
            nc.gpsimd.tensor_tensor(
                out=h_grouped_of[step][:, half * P : (half + 1) * P, :],
                in0=h_sum[:],
                in1=bias[:, col : col + P].unsqueeze(2).to_broadcast([P, P, TOKEN_TILES]),
                op=ADD,
            )

        def quantise_h(step):
            quantise(h_ready[step], 0, h_grouped_of[step].rearrange("p c j -> p (c j)"))

        by_quadrant = out.rearrange("b (hg i) r d -> i r b hg d", i=HEADS_PER_PASS)

        def store(first_hg, groups, heads=range(HEADS_PER_PASS)):
            for i in heads:
                for hg in range(first_hg, first_hg + groups):
                    nc.sync.dma_start(
                        out=by_quadrant[i][:, :, hg, :],
                        in_=result[i * SLOTS : (i + 1) * SLOTS, :, hg, i * HEAD_DIM : (i + 1) * HEAD_DIM],
                    )

        store_after = {(1, 1, 1): (0, 2), (2, 1, 0): (2, 1), (2, 1, 1): (3, 1)}

        def compress(step):
            c, b, blk = step
            hg = 2 * (c - 1) + blk
            kc = psum_flip.tile([P, BLOCK], F32, tag="flipped")
            mx_pass(kc[:], h_ready[(0, b, c - 1)], blk * P, h_ready[step], 0, BLOCK, True, True)
            nc.scalar.copy(out=result[:, b, hg, :], in_=kc[:])
            if step in store_after:
                store(*store_after[step])

        def quantise_h_half(step, half):
            quantise(
                h_ready[step], half * P, h_grouped_of[step][:, half * P : (half + 1) * P, :].rearrange("p c j -> p (c j)")
            )

        def compress_half(step, half):
            c, b, blk = step
            hg = 2 * (c - 1) + blk
            kc = psum_flip.tile([P, P], F32, tag="flipped")
            mx_pass(kc[:], h_ready[(0, b, c - 1)], blk * P, h_ready[step], half * P, P, True, True)
            nc.scalar.copy(out=result[:, b, hg, half * P : (half + 1) * P], in_=kc[:])
            store(hg, 1, (2 * half, 2 * half + 1))

        vector_copy = nc.vector.tensor_copy
        scalar_copy = nc.scalar.copy

        steps = [(c, b, blk) for c in range(2) for b in range(BATCH) for blk in range(CHUNK // BLOCK)]
        steps += [(2, b, blk) for blk in range(CHUNK // BLOCK) for b in range(BATCH)]
        turned = {6: (1,), 8: (1,), 10: (1,)}

        def mm(n):
            halves = turned.get(n, ())
            for half in halves:
                project_channels(steps[n], half)
                add_channel_bias(steps[n], half)
            rest = [half for half in range(2) if half not in halves]
            for i, half in enumerate(rest):
                project(steps[n], half)
                if i == 0:
                    turn(n - 1)
            if not rest:
                turn(n - 1)

        def turn(n):
            for half in turned.get(n, ()):
                turn_half(steps[n], half, scalar_copy)

        def mm_pair(n, pair):
            tiles = range(2 * pair, 2 * pair + 2)
            for half in range(2):
                if half in turned.get(n, ()):
                    project_channels(steps[n], half, tiles)
                    if pair == 1:
                        add_channel_bias(steps[n], half)
                else:
                    project(steps[n], half, tiles)

        def add(n):
            for half in range(2):
                if half not in turned.get(n, ()):
                    add_bias(steps[n], half)

        def hq(n):
            quantise_h(steps[n])

        warm = psum_flip.tile([P, 2 * PASSES, P], F32, tag="flipped")
        for i in range(16):
            nc.tensor.transpose(warm[:, i % 4, :], identity[:], identity[:])
        regroup(0, 0, 0, vector_copy)
        regroup(0, 1, 0, vector_copy)
        transpose_tile(0, 0, 0)
        transpose_tile(0, 0, 1)
        spread_bias(0)
        spread_bias(1)
        spread_bias(2)
        turn_bias(
            [
                c * (CHUNK // P) + blk * (BLOCK // P) + half
                for c, blk, half in sorted({(steps[n][0], steps[n][2], half) for n in turned for half in turned[n]})
            ]
        )
        quantise_w_pass(0, 0, 0)
        quantise_w_pass(0, 1, 0)
        regroup(0, 0, 1, vector_copy)
        quantise_x_pair(0, 0, 0)
        quantise_w_pass(0, 0, 1)
        transpose_tile(0, 0, 2)
        transpose_tile(0, 0, 3)
        quantise_x_tile(0, 0, 2)
        quantise_x_tile(0, 0, 3)
        regroup(0, 1, 1, vector_copy)
        transpose_tile(0, 1, 0)
        mm(0)
        transpose_tile(0, 1, 1)
        transpose_tile(0, 1, 2)
        transpose_tile(0, 1, 3)
        add(0)
        quantise_w_pass(0, 1, 1)
        mm(1)
        regroup(1, 0, 0, scalar_copy)
        quantise_x_pair(0, 1, 0)
        add_bias(steps[1], 0)
        quantise_x_pair(0, 1, 1)
        add_bias(steps[1], 1)
        hq(0)
        regroup(1, 0, 1, scalar_copy)
        transpose_tile(1, 0, 0)
        mm(2)
        transpose_tile(1, 0, 1)
        transpose_tile(1, 0, 2)
        transpose_tile(1, 0, 3)
        mm(3)
        add(2)
        quantise_w(1, 0)
        hq(1)
        quantise_x_pair(1, 0, 0)
        regroup(1, 1, 0, scalar_copy)
        regroup(1, 1, 1, scalar_copy)
        transpose_tile(1, 1, 0)
        transpose_tile(1, 1, 1)
        mm_pair(4, 0)
        quantise_x_pair(1, 0, 1)
        mm_pair(4, 1)
        add(3)
        hq(2)
        transpose_tile(1, 1, 2)
        transpose_tile(1, 1, 3)
        quantise_w(1, 1)
        mm(5)
        add(4)
        hq(3)
        quantise_x_pair(1, 1, 0)
        quantise_x_pair(1, 1, 1)
        regroup(2, 0, 0, scalar_copy)
        regroup(2, 0, 1, scalar_copy)
        mm(6)
        regroup(2, 1, 0, scalar_copy)
        regroup(2, 1, 1, scalar_copy)
        add(5)
        hq(4)
        mm(7)
        add(6)
        hq(5)
        quantise_w(2, 0)
        compress(steps[4])
        mm(8)
        add(7)
        hq(6)
        mm(9)
        compress(steps[5])
        compress(steps[6])
        add(8)
        hq(7)
        quantise_w(2, 1)
        mm(10)
        compress(steps[7])
        add(9)
        hq(8)
        mm(11)
        compress(steps[8])
        add(10)
        hq(9)
        compress(steps[9])
        add_bias(steps[11], 0)
        hq(10)
        add_bias(steps[11], 1)
        compress(steps[10])
        quantise_h_half(steps[11], 0)
        quantise_h_half(steps[11], 1)
        compress_half(steps[11], 0)
        compress_half(steps[11], 1)
